import numpy as np
import ml_dtypes


def mxq(x, axis, fmt="e4m3"):
    dtype, down = {"e4m3": (ml_dtypes.float8_e4m3fn, 7), "e5m2": (ml_dtypes.float8_e5m2, 14)}[fmt]
    v = np.moveaxis(np.asarray(x, np.float32).astype(ml_dtypes.bfloat16).astype(np.float64), axis, -1)
    blocks = v.reshape(v.shape[:-1] + (-1, 32))
    amax = np.abs(blocks).max(-1, keepdims=True)
    byte = np.maximum(np.where(amax > 0, np.frexp(amax)[1] - 1 + 127, 0) - down, 1)
    scale = np.exp2(byte - 127.0)
    codes = (blocks / scale).astype(np.float32).astype(dtype).astype(np.float64)
    return np.moveaxis((codes * scale).reshape(v.shape), -1, axis)


WIDE = False


def mx_kscale(k):
    if not WIDE:
        return np.ones(k)
    levels = np.array([10, -10, 5, -5, 0])
    if k % 512:
        return np.exp2(np.random.permutation(np.resize(levels, k // 32))).repeat(32)
    a = np.empty((k // 512, 16))
    for p in range(k // 512):
        a[p, :8] = np.random.permutation(np.resize(levels, 8))
        for g in range(8):
            far = levels[np.abs(levels - a[p, g]) >= 10]
            a[p, g + 8] = far[np.random.randint(len(far))]
    return np.exp2(a.ravel()).repeat(32)


BF16 = ml_dtypes.bfloat16


def bf(x):
    return np.asarray(x, np.float32).astype(BF16)


def f64(x):
    return np.asarray(x).astype(np.float64)


B, S, D, H, HD, M, G = 4, 768, 1536, 12, 128, 6144, 3
EPS = 1e-6
HH = H * HD


def silu(v):
    return v / (1.0 + np.exp(-v))


def rmsnorm(x, gain):
    var = np.mean(np.square(x), axis=-1, keepdims=True)
    return x * (1.0 / np.sqrt(var + EPS)) * gain


def setup_inputs():
    s, t = mx_kscale(HH), mx_kscale(D)
    return {"attn": bf(0.3 * np.random.standard_normal((B, S, HH)) * s),
            "x": bf(np.random.standard_normal((B, S, D))),
            "w_o": bf(np.random.standard_normal((HH, D)) * 2.0 / np.sqrt(HH) / s[:, None]),
            "rms2_scale": bf((1.0 + 0.1 * np.random.standard_normal(D)) * t),
            "w_gate": bf(np.random.standard_normal((D, M)) / np.sqrt(D) / t[:, None]),
            "w_up": bf(np.random.standard_normal((D, M)) / np.sqrt(D) / t[:, None])}


def reference(attn, x, w_o, rms2_scale, w_gate, w_up):
    x_mid = f64(x) + (mxq(f64(attn), 2, "e4m3") @ mxq(f64(w_o), 0, "e4m3"))
    hq = mxq(rmsnorm(x_mid, f64(rms2_scale)), 2, "e4m3")
    g = silu(hq @ mxq(f64(w_gate), 0, "e4m3")) * (hq @ mxq(f64(w_up), 0, "e4m3"))
    return x_mid, g

@@ -1,0 +1,340 @@
+from contextlib import ExitStack
+
+import concourse.mybir as mybir
+from concourse.masks import make_identity
+
+F32 = mybir.dt.float32
+BF16 = mybir.dt.bfloat16
+U32 = mybir.dt.uint32
+U8 = mybir.dt.uint8
+FP8X4 = mybir.dt.float8_e4m3fn_x4
+ALU = mybir.AluOpType
+ACT = mybir.ActivationFunctionType
+
+TOKENS, D, M = 3072, 1536, 6144
+EPS = 1e-6
+FLOPS = 2 * TOKENS * D * D + 2 * 2 * TOKENS * D * M
+
+P = 128
+PACK = 4
+K_PASS = P * PACK
+PASSES = D // K_PASS
+NT = TOKENS // P
+CH = 512
+NCH = M // CH
+NWO = D // CH
+
+LAGS = (6,)
+DN = 2
+BG_RAMP = "s"
+BG_WOVEN = "s"
+BG_REST = "v"
+LEAD = 6
+RAW_BUFS = 6
+CODE_BUFS = 24
+SG_BUFS = 6
+
+
+def tile_transformerblocktpu_pb_l_kernel(tc, attn, x, w_o, rms2_scale, w_gate, w_up, out_0, out_1):
+    nc = tc.nc
+    attn2 = attn.flatten_outer_dims()
+    x2 = x.flatten_outer_dims()
+    xmid_out = out_0.flatten_outer_dims()
+    g_out = out_1.flatten_outer_dims()
+
+    with ExitStack() as ctx:
+        const = ctx.enter_context(tc.tile_pool(name="const", bufs=1))
+        hpool = ctx.enter_context(tc.tile_pool(name="hcodes", bufs=1))
+        wpool = ctx.enter_context(tc.tile_pool(name="weights", bufs=1))
+        apool = ctx.enter_context(tc.tile_pool(name="stage1", bufs=1))
+        opool = ctx.enter_context(tc.tile_pool(name="outs", bufs=1))
+        psum = ctx.enter_context(tc.psum_pool(name="psum", bufs=8))
+        ctx.enter_context(tc.manual_schedule())
+
+        def bank():
+            return psum.tile([P, CH], F32, name="bank")
+
+        ident = const.tile([P, P], F32, name="ident")
+        make_identity(nc, ident[:])
+        ones = const.tile([P, P], BF16, name="ones")
+        nc.gpsimd.memset(ones[:], 1.0)
+        neg_half = const.tile([P, 1], F32, name="neg_half")
+        nc.gpsimd.memset(neg_half[:], -0.5)
+        gain_row = const.tile([P, D], BF16, name="gain_row")
+        nc.gpsimd.memset(gain_row[:], 0.0)
+        gain_bc = const.tile([P, D], BF16, name="gain_bc")
+        junk = const.tile([P, D], BF16, name="junk")
+        warm = const.tile([P, 1], F32, name="warm")
+        nc.scalar.activation(out=warm[:], in_=neg_half[:], func=ACT.Silu)
+
+        units = {}
+        planes = {}
+
+        def unit_src(key):
+            mat, c, g = key
+            w = {"o": w_o, "g": w_gate, "u": w_up}[mat]
+            return w[g * K_PASS:(g + 1) * K_PASS, c * CH:(c + 1) * CH].rearrange("(p j) w -> p j w", j=PACK)
+
+        def unit_load(key):
+            raw = wpool.tile([P, PACK, CH], BF16, name="wraw", bufs=RAW_BUFS)
+            nc.sync.dma_start(out=raw[:], in_=unit_src(key))
+            units[key] = {"raw": raw}
+
+        def unit_group(key, eng, lo, hi):
+            u = units[key]
+            if "grp" not in u:
+                u["grp"] = wpool.tile([P, CH, PACK], BF16, name="wgrp", bufs=3, align_bytes=64)
+            dst = u["grp"][:, lo:hi, :]
+            src = u["raw"][:, :, lo:hi].rearrange("p j w -> p w j")
+            if eng == "v":
+                nc.vector.tensor_copy(out=dst, in_=src)
+            elif eng == "s":
+                nc.scalar.copy(out=dst, in_=src)
+            else:
+                nc.gpsimd.tensor_scalar(out=dst, in0=src, scalar1=1.0, scalar2=0.0, op0=ALU.mult, op1=ALU.add)
+
+        def unit_quant(key):
+            u = units[key]
+            mat, c, g = key
+            if (mat, c) not in planes:
+                planes[(mat, c)] = wpool.tile([P, CH], U8, name="wscale", bufs=CODE_BUFS // PASSES, align_bytes=64)
+            u["codes"] = wpool.tile([P, CH], U32, name="wcode", bufs=CODE_BUFS, align_bytes=64)
+            u["scales"] = planes[(mat, c)][PACK * g:P, :]
+            nc.vector.quantize_mx(out=u["codes"][:].bitcast(FP8X4), scales=u["scales"],
+                                  in_=u["grp"][:].rearrange("p w j -> p (w j)"))
+
+        araw, xraw, xmid, hb, ga, gh, acod, asca, hcod, hsca, rstd = {}, {}, {}, {}, {}, {}, {}, {}, {}, {}, {}
+
+        def load_attn(i):
+            araw[i] = apool.tile([P, D], BF16, name="araw", bufs=3)
+            nc.sync.dma_start(out=araw[i][:], in_=attn2[i * P:(i + 1) * P, :])
+
+        def load_x(i):
+            xraw[i] = apool.tile([P, D], BF16, name="xraw", bufs=3)
+            nc.sync.dma_start(out=xraw[i][:], in_=x2[i * P:(i + 1) * P, :])
+
+        def transposes(srcs):
+            items = [(s, g) for s in range(len(srcs)) for g in range(PASSES)]
+            for b0 in range(0, len(items), 2):
+                pair = items[b0:b0 + 2]
+                bk = bank()
+                bv = bk[:].rearrange("p (q r) -> p q r", r=P)
+                for q, (s, g) in enumerate(pair):
+                    words = srcs[s][0][:].bitcast(F32)
+                    for u in range(2):
+                        nc.tensor.transpose(bv[:, 2 * q + u, :], words[:, 256 * g + u:256 * (g + 1):2], ident[:])
+                if len(pair) == 2 and pair[0][0] == pair[1][0]:
+                    jobs = [(pair[0][0], pair[0][1], 2, 0)]
+                else:
+                    jobs = [(s, g, 1, q) for q, (s, g) in enumerate(pair)]
+                for s, g, n, q in jobs:
+                    dst = srcs[s][1][:].bitcast(F32)[:, g:g + n, :, :]
+                    src = bv[:, 2 * q:2 * (q + n), :].rearrange("p (g u) r -> p g r u", u=2)
+                    nc.scalar.copy(out=dst, in_=src)
+
+        def quant_tokens(grp, codes, scales):
+            for g in range(PASSES):
+                nc.vector.quantize_mx(out=codes[:, g, :].bitcast(FP8X4), scales=scales[PACK * g:P, :],
+                                      in_=grp[:, g, :, :].rearrange("p r t -> p (r t)"))
+
+        def new_ga(i):
+            ga[i] = apool.tile([P, PASSES, P, PACK], BF16, name="ga", bufs=2, align_bytes=64)
+            return (araw[i], ga[i])
+
+        def new_gh(i):
+            gh[i] = apool.tile([P, PASSES, P, PACK], BF16, name="gh", bufs=2, align_bytes=64)
+            return (hb[i], gh[i])
+
+        def quant_attn(i):
+            acod[i] = apool.tile([P, PASSES, P], U32, name="acod", bufs=3, align_bytes=64)
+            asca[i] = apool.tile([P, P], U8, name="asca", bufs=3, align_bytes=64)
+            quant_tokens(ga[i], acod[i], asca[i])
+
+        def quant_h(i):
+            hcod[i] = hpool.tile([P, PASSES, P], U32, name="hcod%d" % i, align_bytes=64)
+            hsca[i] = hpool.tile([P, P], U8, name="hsca%d" % i, align_bytes=64)
+            quant_tokens(gh[i], hcod[i], hsca[i])
+
+        def mx_pass(out, lcod, lsca, key):
+            g = key[2]
+            u = units[key]
+            nc.tensor.matmul_mx(out=out[:], lhsT=lcod[:, g, :].bitcast(FP8X4), lhsT_scale=lsca[PACK * g:P, :],
+                                rhs=u["codes"][:].bitcast(FP8X4), rhs_scale=u["scales"],
+                                start=(g == 0), stop=(g == PASSES - 1))
+
+        def mx_group(out, lcod, lsca, keys):
+            for key in keys:
+                mx_pass(out, lcod, lsca, key)
+
+        s1bank = {}
+
+        def stage1_mm(i):
+            for n in range(NWO):
+                s1bank[(i, n)] = bank()
+                mx_group(s1bank[(i, n)], acod[i], asca[i], [("o", n, g) for g in range(PASSES)])
+
+        def stage1_add(i, n):
+            if n == 0:
+                xmid[i] = apool.tile([P, D], F32, name="xmid", bufs=4)
+            cols = slice(n * CH, (n + 1) * CH)
+            nc.vector.tensor_tensor(out=xmid[i][:, cols], in0=s1bank[(i, n)][:], in1=xraw[i][:, cols], op=ALU.add)
+
+        def mean_square(i):
+            ssq = apool.tile([P, 1], F32, name="ssq", bufs=4)
+            nc.scalar.activation(out=junk[:], in_=xmid[i][:], func=ACT.Square, accum_out=ssq[:])
+            ms = apool.tile([P, 1], F32, name="ms", bufs=4)
+            nc.gpsimd.tensor_scalar(out=ms[:], in0=ssq[:], scalar1=1.0 / D, scalar2=EPS, op0=ALU.mult, op1=ALU.add)
+            rstd[i] = apool.tile([P, 1], F32, name="rstd", bufs=4)
+            nc.gpsimd.tensor_tensor(out=rstd[i][:], in0=ms[:], in1=neg_half[:], op=ALU.pow)
+
+        def norm(i, g):
+            if g == 0:
+                hb[i] = apool.tile([P, D], BF16, name="hb", bufs=2)
+            cols = slice(g * K_PASS, (g + 1) * K_PASS)
+            nc.vector.scalar_tensor_tensor(out=hb[i][:, cols], in0=xmid[i][:, cols], scalar=rstd[i][:, 0:1],
+                                           in1=gain_bc[:, cols], op0=ALU.mult, op1=ALU.mult)
+
+        def stage2_mm(c, i):
+            bg, bu = bank(), bank()
+            mx_group(bg, hcod[i], hsca[i], [("g", c, g) for g in range(PASSES)])
+            mx_group(bu, hcod[i], hsca[i], [("u", c, g) for g in range(PASSES)])
+            return bg, bu
+
+        def stage2_silu(bg):
+            sg = opool.tile([P, CH], F32, name="sg", bufs=SG_BUFS)
+            nc.scalar.activation(out=sg[:], in_=bg[:], func=ACT.Silu)
+            return sg
+
+        def stage2_mul_store(c, i, bu, sg):
+            nc.vector.tensor_tensor(out=sg[:], in0=bu[:], in1=sg[:], op=ALU.mult)
+            nc.sync.dma_start(out=g_out[i * P:(i + 1) * P, c * CH:(c + 1) * CH], in_=sg[:])
+
+        stream = [(m, c, g) for c in range(NCH) for m in ("g", "u") for g in range(PASSES)]
+        pos = {"load": 0, "item": 0, "live": NWO * PASSES, "turn": 0}
+
+        def bg_load():
+            if pos["load"] < len(stream):
+                unit_load(stream[pos["load"]])
+                pos["load"] += 1
+
+        def bg_item(engines):
+            k = pos["item"]
+            if k > 4 * len(stream):
+                return
+            u, part = k // 4, k % 4
+            if part == 0 and pos["live"] >= CODE_BUFS:
+                return
+            if part == 0 and u >= 1:
+                unit_quant(stream[u - 1])
+                pos["live"] += 1
+            elif part in (1, 2) and u < len(stream):
+                eng = engines[pos["turn"] % len(engines)]
+                pos["turn"] += 1
+                unit_group(stream[u], eng, (part - 1) * CH // 2, part * CH // 2)
+            elif part == 3:
+                bg_load()
+            pos["item"] += 1
+
+        def need_chunk(c, engines):
+            while pos["item"] < 24 * (c + 1) + 1:
+                bg_item(engines)
+
+        wo_units = [("o", n, g) for g in range(PASSES) for n in range(NWO)]
+        load_attn(0)
+        load_attn(1)
+        for key in wo_units[0:RAW_BUFS]:
+            unit_load(key)
+        transposes([new_ga(0), new_ga(1)])
+        for i in range(2):
+            for n in range(NWO):
+                s1bank[(i, n)] = bank()
+        for k in range(len(wo_units) + 1):
+            if k < len(wo_units):
+                unit_group(wo_units[k], "v", 0, CH // 2)
+                unit_group(wo_units[k], "s", CH // 2, CH)
+            if k + RAW_BUFS < len(wo_units):
+                unit_load(wo_units[k + RAW_BUFS])
+            if k == 1:
+                quant_attn(0)
+                quant_attn(1)
+            if k >= 1:
+                unit_quant(wo_units[k - 1])
+                for i in range(2):
+                    mx_pass(s1bank[(i, wo_units[k - 1][1])], acod[i], asca[i], wo_units[k - 1])
+        load_x(0)
+        load_attn(2)
+        load_x(1)
+        nc.sync.dma_start(out=gain_row[0:1, :], in_=rms2_scale.rearrange("(o d) -> o d", o=1))
+        bg_load()
+        bg_load()
+
+        done = {}
+        for i in range(NT + DN + 1):
+            if i + 3 < NT:
+                load_attn(i + 3)
+            if i + 2 < NT:
+                load_x(i + 2)
+            if i < RAW_BUFS - 2:
+                bg_load()
+            now = [(c, i - lag) for c, lag in enumerate(LAGS) if 0 <= i - lag < NT and i - lag <= i - DN - 2]
+            for c, t in now:
+                need_chunk(c, BG_RAMP)
+            if 0 <= i - 1 < NT:
+                mean_square(i - 1)
+            if i < LAGS[0]:
+                for rep in range(24 // LAGS[0]):
+                    bg_item(BG_RAMP)
+            else:
+                for rep in range(len(LAGS) + (1 if i < LAGS[0] + LEAD else 0)):
+                    bg_item(BG_WOVEN)
+            if 2 <= i < NT:
+                stage1_mm(i)
+            for g in range(PASSES):
+                if 0 <= i - DN < NT:
+                    norm(i - DN, g)
+            if i < NT:
+                stage1_add(i, 0)
+            if 1 <= i and i + 1 < NT:
+                quant_attn(i + 1)
+            if i < NT:
+                stage1_add(i, 1)
+            if 0 <= i - DN - 1 < NT:
+                quant_h(i - DN - 1)
+            if i < NT:
+                stage1_add(i, 2)
+                nc.sync.dma_start(out=xmid_out[i * P:(i + 1) * P, :], in_=xmid[i][:])
+            if i == NT - 1:
+                pos["live"] -= NWO * PASSES
+            held = []
+            for c, t in now:
+                bg, bu = stage2_mm(c, t)
+                held.append((c, t, bu, stage2_silu(bg)))
+                done[(c, t)] = True
+                if t == NT - 1:
+                    pos["live"] -= 2 * PASSES
+            for job in held:
+                stage2_mul_store(*job)
+            srcs = []
+            if i + 2 < NT:
+                srcs.append(new_ga(i + 2))
+            if 0 <= i - DN < NT:
+                srcs.append(new_gh(i - DN))
+            if srcs:
+                transposes(srcs)
+            if i == 0:
+                for n in range(NWO):
+                    gb = bank()
+                    nc.tensor.matmul(out=gb[:], lhsT=ones[:], rhs=gain_row[:, n * CH:(n + 1) * CH], start=True, stop=True)
+                    nc.scalar.copy(out=gain_bc[:, n * CH:(n + 1) * CH], in_=gb[:])
+
+        for c in range(NCH):
+            for t in range(NT):
+                if (c, t) in done:
+                    continue
+                need_chunk(c, BG_REST)
+                bg, bu = stage2_mm(c, t)
+                sg = stage2_silu(bg)
+                stage2_mul_store(c, t, bu, sg)
+                if t == NT - 1:
+                    pos["live"] -= 2 * PASSES
+                bg_item(BG_REST)

@@ -24,11 +24,12 @@ CH = 512
 NCH = M // CH
 NWO = D // CH
 
-LAGS = (6,)
+LAGS = (8,)
 DN = 2
-BG_RAMP = "s"
+BG_RAMP = "ssv"
 BG_WOVEN = "s"
-BG_REST = "v"
+BG_REST = "vs"
+BG_START = 2
 LEAD = 6
 RAW_BUFS = 6
 CODE_BUFS = 24
@@ -106,11 +107,11 @@ def tile_transformerblocktpu_pb_l_kernel(tc, attn, x, w_o, rms2_scale, w_gate, w
         araw, xraw, xmid, hb, ga, gh, acod, asca, hcod, hsca, rstd = {}, {}, {}, {}, {}, {}, {}, {}, {}, {}, {}
 
         def load_attn(i):
-            araw[i] = apool.tile([P, D], BF16, name="araw", bufs=3)
+            araw[i] = apool.tile([P, D], BF16, name="araw", bufs=4)
             nc.sync.dma_start(out=araw[i][:], in_=attn2[i * P:(i + 1) * P, :])
 
         def load_x(i):
-            xraw[i] = apool.tile([P, D], BF16, name="xraw", bufs=3)
+            xraw[i] = apool.tile([P, D], BF16, name="xraw", bufs=4)
             nc.sync.dma_start(out=xraw[i][:], in_=x2[i * P:(i + 1) * P, :])
 
         def transposes(srcs):
@@ -122,7 +123,11 @@ def tile_transformerblocktpu_pb_l_kernel(tc, attn, x, w_o, rms2_scale, w_gate, w
                 for q, (s, g) in enumerate(pair):
                     words = srcs[s][0][:].bitcast(F32)
                     for u in range(2):
-                        nc.tensor.transpose(bv[:, 2 * q + u, :], words[:, 256 * g + u:256 * (g + 1):2], ident[:])
+                        if srcs[s][2]:
+                            in_words = words[:, 256 * g + P * u:256 * g + P * (u + 1)]
+                        else:
+                            in_words = words[:, 256 * g + u:256 * (g + 1):2]
+                        nc.tensor.transpose(bv[:, 2 * q + u, :], in_words, ident[:])
                 if len(pair) == 2 and pair[0][0] == pair[1][0]:
                     jobs = [(pair[0][0], pair[0][1], 2, 0)]
                 else:
@@ -139,15 +144,15 @@ def tile_transformerblocktpu_pb_l_kernel(tc, attn, x, w_o, rms2_scale, w_gate, w
 
         def new_ga(i):
             ga[i] = apool.tile([P, PASSES, P, PACK], BF16, name="ga", bufs=2, align_bytes=64)
-            return (araw[i], ga[i])
+            return (araw[i], ga[i], False)
 
         def new_gh(i):
             gh[i] = apool.tile([P, PASSES, P, PACK], BF16, name="gh", bufs=2, align_bytes=64)
-            return (hb[i], gh[i])
+            return (hb[i], gh[i], True)
 
         def quant_attn(i):
-            acod[i] = apool.tile([P, PASSES, P], U32, name="acod", bufs=3, align_bytes=64)
-            asca[i] = apool.tile([P, P], U8, name="asca", bufs=3, align_bytes=64)
+            acod[i] = apool.tile([P, PASSES, P], U32, name="acod", bufs=4, align_bytes=64)
+            asca[i] = apool.tile([P, P], U8, name="asca", bufs=4, align_bytes=64)
             quant_tokens(ga[i], acod[i], asca[i])
 
         def quant_h(i):
@@ -162,16 +167,14 @@ def tile_transformerblocktpu_pb_l_kernel(tc, attn, x, w_o, rms2_scale, w_gate, w
                                 rhs=u["codes"][:].bitcast(FP8X4), rhs_scale=u["scales"],
                                 start=(g == 0), stop=(g == PASSES - 1))
 
-        def mx_group(out, lcod, lsca, keys):
-            for key in keys:
-                mx_pass(out, lcod, lsca, key)
-
         s1bank = {}
 
         def stage1_mm(i):
             for n in range(NWO):
                 s1bank[(i, n)] = bank()
-                mx_group(s1bank[(i, n)], acod[i], asca[i], [("o", n, g) for g in range(PASSES)])
+            for g in range(PASSES):
+                for n in range(NWO):
+                    mx_pass(s1bank[(i, n)], acod[i], asca[i], ("o", n, g))
 
         def stage1_add(i, n):
             if n == 0:
@@ -191,13 +194,18 @@ def tile_transformerblocktpu_pb_l_kernel(tc, attn, x, w_o, rms2_scale, w_gate, w
             if g == 0:
                 hb[i] = apool.tile([P, D], BF16, name="hb", bufs=2)
             cols = slice(g * K_PASS, (g + 1) * K_PASS)
-            nc.vector.scalar_tensor_tensor(out=hb[i][:, cols], in0=xmid[i][:, cols], scalar=rstd[i][:, 0:1],
-                                           in1=gain_bc[:, cols], op0=ALU.mult, op1=ALU.mult)
+            xs = xmid[i][:, cols].rearrange("p (q u e) -> p u q e", u=2, e=2)
+            for u in range(2):
+                half = slice(g * K_PASS + u * 2 * P, g * K_PASS + (u + 1) * 2 * P)
+                nc.vector.scalar_tensor_tensor(out=hb[i][:, half].rearrange("p (q e) -> p q e", e=2), in0=xs[:, u, :, :],
+                                               scalar=rstd[i][:, 0:1], in1=gain_bc[:, half].rearrange("p (q e) -> p q e", e=2),
+                                               op0=ALU.mult, op1=ALU.mult)
 
         def stage2_mm(c, i):
             bg, bu = bank(), bank()
-            mx_group(bg, hcod[i], hsca[i], [("g", c, g) for g in range(PASSES)])
-            mx_group(bu, hcod[i], hsca[i], [("u", c, g) for g in range(PASSES)])
+            for g in range(PASSES):
+                mx_pass(bg, hcod[i], hsca[i], ("g", c, g))
+                mx_pass(bu, hcod[i], hsca[i], ("u", c, g))
             return bg, bu
 
         def stage2_silu(bg):
@@ -240,10 +248,14 @@ def tile_transformerblocktpu_pb_l_kernel(tc, attn, x, w_o, rms2_scale, w_gate, w
                 bg_item(engines)
 
         wo_units = [("o", n, g) for g in range(PASSES) for n in range(NWO)]
+        early = {0: lambda: load_attn(2), 3: lambda: load_x(0), 4: lambda: load_attn(3), 6: lambda: load_x(1)}
         load_attn(0)
         load_attn(1)
-        for key in wo_units[0:RAW_BUFS]:
-            unit_load(key)
+        nload = 0
+        for k in range(RAW_BUFS):
+            unit_load(wo_units[k])
+            if k in early:
+                early[k]()
         transposes([new_ga(0), new_ga(1)])
         for i in range(2):
             for n in range(NWO):
@@ -254,35 +266,40 @@ def tile_transformerblocktpu_pb_l_kernel(tc, attn, x, w_o, rms2_scale, w_gate, w
                 unit_group(wo_units[k], "s", CH // 2, CH)
             if k + RAW_BUFS < len(wo_units):
                 unit_load(wo_units[k + RAW_BUFS])
+                if k + RAW_BUFS in early:
+                    early[k + RAW_BUFS]()
             if k == 1:
                 quant_attn(0)
                 quant_attn(1)
+            if k in (3, 5):
+                transposes([new_ga(2 + (k - 3) // 2)])
+            if k in (5, 7):
+                quant_attn(2 + (k - 5) // 2)
             if k >= 1:
                 unit_quant(wo_units[k - 1])
                 for i in range(2):
                     mx_pass(s1bank[(i, wo_units[k - 1][1])], acod[i], asca[i], wo_units[k - 1])
-        load_x(0)
-        load_attn(2)
-        load_x(1)
         nc.sync.dma_start(out=gain_row[0:1, :], in_=rms2_scale.rearrange("(o d) -> o d", o=1))
-        bg_load()
-        bg_load()
+        load_x(2)
+        load_attn(4)
 
         done = {}
         for i in range(NT + DN + 1):
+            if i + 5 < NT:
+                load_attn(i + 5)
             if i + 3 < NT:
-                load_attn(i + 3)
-            if i + 2 < NT:
-                load_x(i + 2)
-            if i < RAW_BUFS - 2:
+                load_x(i + 3)
+            if i < RAW_BUFS:
                 bg_load()
             now = [(c, i - lag) for c, lag in enumerate(LAGS) if 0 <= i - lag < NT and i - lag <= i - DN - 2]
             for c, t in now:
                 need_chunk(c, BG_RAMP)
             if 0 <= i - 1 < NT:
                 mean_square(i - 1)
-            if i < LAGS[0]:
-                for rep in range(24 // LAGS[0]):
+            if i < BG_START:
+                pass
+            elif i < LAGS[0]:
+                while pos["item"] * (LAGS[0] - BG_START) < 24 * (i - BG_START + 1):
                     bg_item(BG_RAMP)
             else:
                 for rep in range(len(LAGS) + (1 if i < LAGS[0] + LEAD else 0)):
@@ -294,8 +311,8 @@ def tile_transformerblocktpu_pb_l_kernel(tc, attn, x, w_o, rms2_scale, w_gate, w
                     norm(i - DN, g)
             if i < NT:
                 stage1_add(i, 0)
-            if 1 <= i and i + 1 < NT:
-                quant_attn(i + 1)
+            if 2 <= i and i + 2 < NT:
+                quant_attn(i + 2)
             if i < NT:
                 stage1_add(i, 1)
             if 0 <= i - DN - 1 < NT:
@@ -315,8 +332,8 @@ def tile_transformerblocktpu_pb_l_kernel(tc, attn, x, w_o, rms2_scale, w_gate, w
             for job in held:
                 stage2_mul_store(*job)
             srcs = []
-            if i + 2 < NT:
-                srcs.append(new_ga(i + 2))
+            if 1 <= i and i + 3 < NT:
+                srcs.append(new_ga(i + 3))
             if 0 <= i - DN < NT:
                 srcs.append(new_gh(i - DN))
             if srcs:
@@ -325,7 +342,8 @@ def tile_transformerblocktpu_pb_l_kernel(tc, attn, x, w_o, rms2_scale, w_gate, w
                 for n in range(NWO):
                     gb = bank()
                     nc.tensor.matmul(out=gb[:], lhsT=ones[:], rhs=gain_row[:, n * CH:(n + 1) * CH], start=True, stop=True)
-                    nc.scalar.copy(out=gain_bc[:, n * CH:(n + 1) * CH], in_=gb[:])
+                    nc.scalar.copy(out=gain_bc[:, n * CH:(n + 1) * CH].rearrange("p (u q e) -> p u q e", u=2, e=2),
+                                   in_=gb[:].rearrange("p (q u e) -> p u q e", u=2, e=2))
 
         for c in range(NCH):
             for t in range(NT):

@@ -24,12 +24,11 @@ CH = 512
 NCH = M // CH
 NWO = D // CH
 
-LAGS = (8,)
+LAGS = (6,)
 DN = 2
-BG_RAMP = "ssv"
+BG_RAMP = "s"
 BG_WOVEN = "s"
-BG_REST = "vs"
-BG_START = 2
+BG_REST = "v"
 LEAD = 6
 RAW_BUFS = 6
 CODE_BUFS = 24
@@ -104,77 +103,66 @@ def tile_transformerblocktpu_pb_l_kernel(tc, attn, x, w_o, rms2_scale, w_gate, w
             nc.vector.quantize_mx(out=u["codes"][:].bitcast(FP8X4), scales=u["scales"],
                                   in_=u["grp"][:].rearrange("p w j -> p (w j)"))
 
-        araw, xraw, xmid, hb, ga, gh, acod, asca, hcod, hsca, rstd = {}, {}, {}, {}, {}, {}, {}, {}, {}, {}, {}
+        araw, xraw, xmid, hb, grouped, acod, asca, hcod, hsca, rstd = {}, {}, {}, {}, {}, {}, {}, {}, {}, {}
 
         def load_attn(i):
-            araw[i] = apool.tile([P, D], BF16, name="araw", bufs=4)
+            araw[i] = apool.tile([P, D], BF16, name="araw", bufs=3)
             nc.sync.dma_start(out=araw[i][:], in_=attn2[i * P:(i + 1) * P, :])
 
         def load_x(i):
-            xraw[i] = apool.tile([P, D], BF16, name="xraw", bufs=4)
+            xraw[i] = apool.tile([P, D], BF16, name="xraw", bufs=3)
             nc.sync.dma_start(out=xraw[i][:], in_=x2[i * P:(i + 1) * P, :])
 
         def transposes(srcs):
-            items = [(s, g) for s in range(len(srcs)) for g in range(PASSES)]
+            grp = apool.tile([P, 2 * PASSES, P, PACK], BF16, name="grp", bufs=2, align_bytes=64)
+            gw = grp[:].bitcast(F32)
+            items = [(kind, i, g) for kind, i in srcs for g in range(PASSES)]
+            for s, (kind, i) in enumerate(srcs):
+                grouped[(kind, i)] = grp[:, s * PASSES:(s + 1) * PASSES, :, :]
             for b0 in range(0, len(items), 2):
                 pair = items[b0:b0 + 2]
                 bk = bank()
                 bv = bk[:].rearrange("p (q r) -> p q r", r=P)
-                for q, (s, g) in enumerate(pair):
-                    words = srcs[s][0][:].bitcast(F32)
+                for q, (kind, i, g) in enumerate(pair):
+                    words = (araw[i] if kind == "a" else hb[i])[:].bitcast(F32)
                     for u in range(2):
-                        if srcs[s][2]:
-                            in_words = words[:, 256 * g + P * u:256 * g + P * (u + 1)]
-                        else:
-                            in_words = words[:, 256 * g + u:256 * (g + 1):2]
-                        nc.tensor.transpose(bv[:, 2 * q + u, :], in_words, ident[:])
-                if len(pair) == 2 and pair[0][0] == pair[1][0]:
-                    jobs = [(pair[0][0], pair[0][1], 2, 0)]
-                else:
-                    jobs = [(s, g, 1, q) for q, (s, g) in enumerate(pair)]
-                for s, g, n, q in jobs:
-                    dst = srcs[s][1][:].bitcast(F32)[:, g:g + n, :, :]
-                    src = bv[:, 2 * q:2 * (q + n), :].rearrange("p (g u) r -> p g r u", u=2)
-                    nc.scalar.copy(out=dst, in_=src)
+                        nc.tensor.transpose(bv[:, 2 * q + u, :], words[:, 256 * g + u:256 * (g + 1):2], ident[:])
+                n = len(pair)
+                nc.scalar.copy(out=gw[:, b0:b0 + n, :, :], in_=bv[:, 0:2 * n, :].rearrange("p (g u) r -> p g r u", u=2))
 
         def quant_tokens(grp, codes, scales):
-            for g in range(PASSES):
-                nc.vector.quantize_mx(out=codes[:, g, :].bitcast(FP8X4), scales=scales[PACK * g:P, :],
-                                      in_=grp[:, g, :, :].rearrange("p r t -> p (r t)"))
-
-        def new_ga(i):
-            ga[i] = apool.tile([P, PASSES, P, PACK], BF16, name="ga", bufs=2, align_bytes=64)
-            return (araw[i], ga[i], False)
-
-        def new_gh(i):
-            gh[i] = apool.tile([P, PASSES, P, PACK], BF16, name="gh", bufs=2, align_bytes=64)
-            return (hb[i], gh[i], True)
+            for lo, hi in ((0, 2), (2, 3)):
+                nc.vector.quantize_mx(out=codes[:, lo:hi, :].rearrange("p g r -> p (g r)").bitcast(FP8X4),
+                                      scales=scales[:, lo * P:hi * P],
+                                      in_=grp[:, lo:hi, :, :].rearrange("p g r t -> p (g r t)"))
 
         def quant_attn(i):
-            acod[i] = apool.tile([P, PASSES, P], U32, name="acod", bufs=4, align_bytes=64)
-            asca[i] = apool.tile([P, P], U8, name="asca", bufs=4, align_bytes=64)
-            quant_tokens(ga[i], acod[i], asca[i])
+            acod[i] = apool.tile([P, PASSES, P], U32, name="acod", bufs=3, align_bytes=64)
+            asca[i] = apool.tile([P, PASSES * P], U8, name="asca", bufs=3, align_bytes=64)
+            quant_tokens(grouped[("a", i)], acod[i], asca[i])
 
         def quant_h(i):
             hcod[i] = hpool.tile([P, PASSES, P], U32, name="hcod%d" % i, align_bytes=64)
-            hsca[i] = hpool.tile([P, P], U8, name="hsca%d" % i, align_bytes=64)
-            quant_tokens(gh[i], hcod[i], hsca[i])
+            hsca[i] = hpool.tile([P, PASSES * P], U8, name="hsca%d" % i, align_bytes=64)
+            quant_tokens(grouped[("h", i)], hcod[i], hsca[i])
 
         def mx_pass(out, lcod, lsca, key):
             g = key[2]
             u = units[key]
-            nc.tensor.matmul_mx(out=out[:], lhsT=lcod[:, g, :].bitcast(FP8X4), lhsT_scale=lsca[PACK * g:P, :],
+            nc.tensor.matmul_mx(out=out[:], lhsT=lcod[:, g, :].bitcast(FP8X4), lhsT_scale=lsca[:, g * P:(g + 1) * P],
                                 rhs=u["codes"][:].bitcast(FP8X4), rhs_scale=u["scales"],
                                 start=(g == 0), stop=(g == PASSES - 1))
+
+        def mx_group(out, lcod, lsca, keys):
+            for key in keys:
+                mx_pass(out, lcod, lsca, key)
 
         s1bank = {}
 
         def stage1_mm(i):
             for n in range(NWO):
                 s1bank[(i, n)] = bank()
-            for g in range(PASSES):
-                for n in range(NWO):
-                    mx_pass(s1bank[(i, n)], acod[i], asca[i], ("o", n, g))
+                mx_group(s1bank[(i, n)], acod[i], asca[i], [("o", n, g) for g in range(PASSES)])
 
         def stage1_add(i, n):
             if n == 0:
@@ -190,22 +178,15 @@ def tile_transformerblocktpu_pb_l_kernel(tc, attn, x, w_o, rms2_scale, w_gate, w
             rstd[i] = apool.tile([P, 1], F32, name="rstd", bufs=4)
             nc.gpsimd.tensor_tensor(out=rstd[i][:], in0=ms[:], in1=neg_half[:], op=ALU.pow)
 
-        def norm(i, g):
-            if g == 0:
-                hb[i] = apool.tile([P, D], BF16, name="hb", bufs=2)
-            cols = slice(g * K_PASS, (g + 1) * K_PASS)
-            xs = xmid[i][:, cols].rearrange("p (q u e) -> p u q e", u=2, e=2)
-            for u in range(2):
-                half = slice(g * K_PASS + u * 2 * P, g * K_PASS + (u + 1) * 2 * P)
-                nc.vector.scalar_tensor_tensor(out=hb[i][:, half].rearrange("p (q e) -> p q e", e=2), in0=xs[:, u, :, :],
-                                               scalar=rstd[i][:, 0:1], in1=gain_bc[:, half].rearrange("p (q e) -> p q e", e=2),
-                                               op0=ALU.mult, op1=ALU.mult)
+        def norm(i):
+            hb[i] = apool.tile([P, D], BF16, name="hb", bufs=2)
+            nc.vector.scalar_tensor_tensor(out=hb[i][:], in0=xmid[i][:], scalar=rstd[i][:, 0:1],
+                                           in1=gain_bc[:], op0=ALU.mult, op1=ALU.mult)
 
         def stage2_mm(c, i):
             bg, bu = bank(), bank()
-            for g in range(PASSES):
-                mx_pass(bg, hcod[i], hsca[i], ("g", c, g))
-                mx_pass(bu, hcod[i], hsca[i], ("u", c, g))
+            mx_group(bg, hcod[i], hsca[i], [("g", c, g) for g in range(PASSES)])
+            mx_group(bu, hcod[i], hsca[i], [("u", c, g) for g in range(PASSES)])
             return bg, bu
 
         def stage2_silu(bg):
@@ -248,15 +229,11 @@ def tile_transformerblocktpu_pb_l_kernel(tc, attn, x, w_o, rms2_scale, w_gate, w
                 bg_item(engines)
 
         wo_units = [("o", n, g) for g in range(PASSES) for n in range(NWO)]
-        early = {0: lambda: load_attn(2), 3: lambda: load_x(0), 4: lambda: load_attn(3), 6: lambda: load_x(1)}
         load_attn(0)
         load_attn(1)
-        nload = 0
-        for k in range(RAW_BUFS):
-            unit_load(wo_units[k])
-            if k in early:
-                early[k]()
-        transposes([new_ga(0), new_ga(1)])
+        for key in wo_units[0:RAW_BUFS]:
+            unit_load(key)
+        transposes([("a", 0), ("a", 1)])
         for i in range(2):
             for n in range(NWO):
                 s1bank[(i, n)] = bank()
@@ -266,53 +243,47 @@ def tile_transformerblocktpu_pb_l_kernel(tc, attn, x, w_o, rms2_scale, w_gate, w
                 unit_group(wo_units[k], "s", CH // 2, CH)
             if k + RAW_BUFS < len(wo_units):
                 unit_load(wo_units[k + RAW_BUFS])
-                if k + RAW_BUFS in early:
-                    early[k + RAW_BUFS]()
             if k == 1:
                 quant_attn(0)
                 quant_attn(1)
-            if k in (3, 5):
-                transposes([new_ga(2 + (k - 3) // 2)])
-            if k in (5, 7):
-                quant_attn(2 + (k - 5) // 2)
             if k >= 1:
                 unit_quant(wo_units[k - 1])
                 for i in range(2):
                     mx_pass(s1bank[(i, wo_units[k - 1][1])], acod[i], asca[i], wo_units[k - 1])
+        load_x(0)
+        load_attn(2)
+        load_x(1)
         nc.sync.dma_start(out=gain_row[0:1, :], in_=rms2_scale.rearrange("(o d) -> o d", o=1))
-        load_x(2)
-        load_attn(4)
+        bg_load()
+        bg_load()
 
         done = {}
         for i in range(NT + DN + 1):
-            if i + 5 < NT:
-                load_attn(i + 5)
             if i + 3 < NT:
-                load_x(i + 3)
-            if i < RAW_BUFS:
+                load_attn(i + 3)
+            if i + 2 < NT:
+                load_x(i + 2)
+            if i < RAW_BUFS - 2:
                 bg_load()
             now = [(c, i - lag) for c, lag in enumerate(LAGS) if 0 <= i - lag < NT and i - lag <= i - DN - 2]
             for c, t in now:
                 need_chunk(c, BG_RAMP)
             if 0 <= i - 1 < NT:
                 mean_square(i - 1)
-            if i < BG_START:
-                pass
-            elif i < LAGS[0]:
-                while pos["item"] * (LAGS[0] - BG_START) < 24 * (i - BG_START + 1):
+            if i < LAGS[0]:
+                for rep in range(24 // LAGS[0]):
                     bg_item(BG_RAMP)
             else:
                 for rep in range(len(LAGS) + (1 if i < LAGS[0] + LEAD else 0)):
                     bg_item(BG_WOVEN)
             if 2 <= i < NT:
                 stage1_mm(i)
-            for g in range(PASSES):
-                if 0 <= i - DN < NT:
-                    norm(i - DN, g)
+            if 0 <= i - DN < NT:
+                norm(i - DN)
             if i < NT:
                 stage1_add(i, 0)
-            if 2 <= i and i + 2 < NT:
-                quant_attn(i + 2)
+            if 1 <= i and i + 1 < NT:
+                quant_attn(i + 1)
             if i < NT:
                 stage1_add(i, 1)
             if 0 <= i - DN - 1 < NT:
@@ -332,18 +303,17 @@ def tile_transformerblocktpu_pb_l_kernel(tc, attn, x, w_o, rms2_scale, w_gate, w
             for job in held:
                 stage2_mul_store(*job)
             srcs = []
-            if 1 <= i and i + 3 < NT:
-                srcs.append(new_ga(i + 3))
+            if i + 2 < NT:
+                srcs.append(("a", i + 2))
             if 0 <= i - DN < NT:
-                srcs.append(new_gh(i - DN))
+                srcs.append(("h", i - DN))
             if srcs:
                 transposes(srcs)
             if i == 0:
                 for n in range(NWO):
                     gb = bank()
                     nc.tensor.matmul(out=gb[:], lhsT=ones[:], rhs=gain_row[:, n * CH:(n + 1) * CH], start=True, stop=True)
-                    nc.scalar.copy(out=gain_bc[:, n * CH:(n + 1) * CH].rearrange("p (u q e) -> p u q e", u=2, e=2),
-                                   in_=gb[:].rearrange("p (q u e) -> p u q e", u=2, e=2))
+                    nc.scalar.copy(out=gain_bc[:, n * CH:(n + 1) * CH], in_=gb[:])
 
         for c in range(NCH):
             for t in range(NT):

@@ -162,7 +162,9 @@ def tile_transformerblocktpu_pb_l_kernel(tc, attn, x, w_o, rms2_scale, w_gate, w
         def stage1_mm(i):
             for n in range(NWO):
                 s1bank[(i, n)] = bank()
-                mx_group(s1bank[(i, n)], acod[i], asca[i], [("o", n, g) for g in range(PASSES)])
+            for g in range(PASSES):
+                for n in range(NWO):
+                    mx_pass(s1bank[(i, n)], acod[i], asca[i], ("o", n, g))
 
         def stage1_add(i, n):
             if n == 0:
@@ -185,8 +187,9 @@ def tile_transformerblocktpu_pb_l_kernel(tc, attn, x, w_o, rms2_scale, w_gate, w
 
         def stage2_mm(c, i):
             bg, bu = bank(), bank()
-            mx_group(bg, hcod[i], hsca[i], [("g", c, g) for g in range(PASSES)])
-            mx_group(bu, hcod[i], hsca[i], [("u", c, g) for g in range(PASSES)])
+            for g in range(PASSES):
+                mx_pass(bg, hcod[i], hsca[i], ("g", c, g))
+                mx_pass(bu, hcod[i], hsca[i], ("u", c, g))
             return bg, bu
 
         def stage2_silu(bg):

@@ -30,6 +30,7 @@ BG_RAMP = "s"
 BG_WOVEN = "s"
 BG_REST = "v"
 LEAD = 6
+ACOD_BUFS = {4: 1, 2: 3, 1: 2}
 RAW_BUFS = 6
 CODE_BUFS = 24
 SG_BUFS = 6
@@ -60,7 +61,7 @@ def tile_transformerblocktpu_pb_l_kernel(tc, attn, x, w_o, rms2_scale, w_gate, w
         nc.gpsimd.memset(ones[:], 1.0)
         neg_half = const.tile([P, 1], F32, name="neg_half")
         nc.gpsimd.memset(neg_half[:], -0.5)
-        gain_row = const.tile([P, D], BF16, name="gain_row")
+        gain_row = apool.tile([P, D], BF16, name="hb", bufs=2)
         nc.gpsimd.memset(gain_row[:], 0.0)
         gain_bc = const.tile([P, D], BF16, name="gain_bc")
         junk = const.tile([P, D], BF16, name="junk")
@@ -103,7 +104,7 @@ def tile_transformerblocktpu_pb_l_kernel(tc, attn, x, w_o, rms2_scale, w_gate, w
             nc.vector.quantize_mx(out=u["codes"][:].bitcast(FP8X4), scales=u["scales"],
                                   in_=u["grp"][:].rearrange("p w j -> p (w j)"))
 
-        araw, xraw, xmid, hb, grouped, acod, asca, hcod, hsca, rstd = {}, {}, {}, {}, {}, {}, {}, {}, {}, {}
+        araw, xraw, xmid, hb, tokcodes, runs, rstd = {}, {}, {}, {}, {}, {}, {}
 
         def load_attn(i):
             araw[i] = apool.tile([P, D], BF16, name="araw", bufs=3)
@@ -117,8 +118,6 @@ def tile_transformerblocktpu_pb_l_kernel(tc, attn, x, w_o, rms2_scale, w_gate, w
             grp = apool.tile([P, 2 * PASSES, P, PACK], BF16, name="grp", bufs=2, align_bytes=64)
             gw = grp[:].bitcast(F32)
             items = [(kind, i, g) for kind, i in srcs for g in range(PASSES)]
-            for s, (kind, i) in enumerate(srcs):
-                grouped[(kind, i)] = grp[:, s * PASSES:(s + 1) * PASSES, :, :]
             for b0 in range(0, len(items), 2):
                 pair = items[b0:b0 + 2]
                 bk = bank()
@@ -129,42 +128,49 @@ def tile_transformerblocktpu_pb_l_kernel(tc, attn, x, w_o, rms2_scale, w_gate, w
                         nc.tensor.transpose(bv[:, 2 * q + u, :], words[:, 256 * g + u:256 * (g + 1):2], ident[:])
                 n = len(pair)
                 nc.scalar.copy(out=gw[:, b0:b0 + n, :, :], in_=bv[:, 0:2 * n, :].rearrange("p (g u) r -> p g r u", u=2))
+            return (grp, items)
 
-        def quant_tokens(grp, codes, scales):
-            for lo, hi in ((0, 2), (2, 3)):
-                nc.vector.quantize_mx(out=codes[:, lo:hi, :].rearrange("p g r -> p (g r)").bitcast(FP8X4),
-                                      scales=scales[:, lo * P:hi * P],
+        def quant_run(run):
+            grp, items = run
+            n = len(items)
+            first = 4 if n == 6 else 2
+            keep = items[0][0] == "h"
+            pool = hpool if keep else apool
+            for lo, hi in ((0, first), (first, n)):
+                w = hi - lo
+                if keep and lo == 0:
+                    cod = hpool.tile([P, w, P], U32, name="hcod%d" % items[0][1], align_bytes=64)
+                    sca = hpool.tile([P, w * P], U8, name="hsca%d" % items[0][1], align_bytes=64)
+                elif keep and n == 3:
+                    cod = hpool.tile([P, w, P], U32, name="hcodb%d" % items[0][1], align_bytes=64)
+                    sca = hpool.tile([P, w * P], U8, name="hscab%d" % items[0][1], align_bytes=64)
+                else:
+                    cod = apool.tile([P, w, P], U32, name="acod%d" % w, bufs=ACOD_BUFS[w], align_bytes=64)
+                    sca = apool.tile([P, w * P], U8, name="asca%d" % w, bufs=ACOD_BUFS[w], align_bytes=64)
+                nc.vector.quantize_mx(out=cod[:].rearrange("p g r -> p (g r)").bitcast(FP8X4), scales=sca[:],
                                       in_=grp[:, lo:hi, :, :].rearrange("p g r t -> p (g r t)"))
+                for s in range(lo, hi):
+                    kind, i, g = items[s]
+                    tokcodes[(kind, i, g)] = (cod[:, s - lo, :], sca[:, (s - lo) * P:(s - lo + 1) * P])
 
-        def quant_attn(i):
-            acod[i] = apool.tile([P, PASSES, P], U32, name="acod", bufs=3, align_bytes=64)
-            asca[i] = apool.tile([P, PASSES * P], U8, name="asca", bufs=3, align_bytes=64)
-            quant_tokens(grouped[("a", i)], acod[i], asca[i])
-
-        def quant_h(i):
-            hcod[i] = hpool.tile([P, PASSES, P], U32, name="hcod%d" % i, align_bytes=64)
-            hsca[i] = hpool.tile([P, PASSES * P], U8, name="hsca%d" % i, align_bytes=64)
-            quant_tokens(grouped[("h", i)], hcod[i], hsca[i])
-
-        def mx_pass(out, lcod, lsca, key):
+        def mx_pass(out, kind, i, key):
             g = key[2]
             u = units[key]
-            nc.tensor.matmul_mx(out=out[:], lhsT=lcod[:, g, :].bitcast(FP8X4), lhsT_scale=lsca[:, g * P:(g + 1) * P],
+            lcod, lsca = tokcodes[(kind, i, g)]
+            nc.tensor.matmul_mx(out=out[:], lhsT=lcod.bitcast(FP8X4), lhsT_scale=lsca,
                                 rhs=u["codes"][:].bitcast(FP8X4), rhs_scale=u["scales"],
                                 start=(g == 0), stop=(g == PASSES - 1))
 
-        def mx_group(out, lcod, lsca, keys):
+        def mx_group(out, kind, i, keys):
             for key in keys:
-                mx_pass(out, lcod, lsca, key)
+                mx_pass(out, kind, i, key)
 
         s1bank = {}
 
         def stage1_mm(i):
             for n in range(NWO):
                 s1bank[(i, n)] = bank()
-            for g in range(PASSES):
-                for n in range(NWO):
-                    mx_pass(s1bank[(i, n)], acod[i], asca[i], ("o", n, g))
+                mx_group(s1bank[(i, n)], "a", i, [("o", n, g) for g in range(PASSES)])
 
         def stage1_add(i, n):
             if n == 0:
@@ -187,9 +193,8 @@ def tile_transformerblocktpu_pb_l_kernel(tc, attn, x, w_o, rms2_scale, w_gate, w
 
         def stage2_mm(c, i):
             bg, bu = bank(), bank()
-            for g in range(PASSES):
-                mx_pass(bg, hcod[i], hsca[i], ("g", c, g))
-                mx_pass(bu, hcod[i], hsca[i], ("u", c, g))
+            mx_group(bg, "h", i, [("g", c, g) for g in range(PASSES)])
+            mx_group(bu, "h", i, [("u", c, g) for g in range(PASSES)])
             return bg, bu
 
         def stage2_silu(bg):
@@ -209,7 +214,14 @@ def tile_transformerblocktpu_pb_l_kernel(tc, attn, x, w_o, rms2_scale, w_gate, w
                 unit_load(stream[pos["load"]])
                 pos["load"] += 1
 
-        def bg_item(engines):
+        pending = {"keys": []}
+
+        def flush():
+            for key in pending["keys"]:
+                unit_quant(key)
+            pending["keys"] = []
+
+        def bg_item(engines, defer=False):
             k = pos["item"]
             if k > 4 * len(stream):
                 return
@@ -217,7 +229,10 @@ def tile_transformerblocktpu_pb_l_kernel(tc, attn, x, w_o, rms2_scale, w_gate, w
             if part == 0 and pos["live"] >= CODE_BUFS:
                 return
             if part == 0 and u >= 1:
-                unit_quant(stream[u - 1])
+                if defer:
+                    pending["keys"] = pending["keys"] + [stream[u - 1]]
+                else:
+                    unit_quant(stream[u - 1])
                 pos["live"] += 1
             elif part in (1, 2) and u < len(stream):
                 eng = engines[pos["turn"] % len(engines)]
@@ -236,7 +251,7 @@ def tile_transformerblocktpu_pb_l_kernel(tc, attn, x, w_o, rms2_scale, w_gate, w
         load_attn(1)
         for key in wo_units[0:RAW_BUFS]:
             unit_load(key)
-        transposes([("a", 0), ("a", 1)])
+        runs[-1] = transposes([("a", 0), ("a", 1)])
         for i in range(2):
             for n in range(NWO):
                 s1bank[(i, n)] = bank()
@@ -247,12 +262,11 @@ def tile_transformerblocktpu_pb_l_kernel(tc, attn, x, w_o, rms2_scale, w_gate, w
             if k + RAW_BUFS < len(wo_units):
                 unit_load(wo_units[k + RAW_BUFS])
             if k == 1:
-                quant_attn(0)
-                quant_attn(1)
+                quant_run(runs[-1])
             if k >= 1:
                 unit_quant(wo_units[k - 1])
                 for i in range(2):
-                    mx_pass(s1bank[(i, wo_units[k - 1][1])], acod[i], asca[i], wo_units[k - 1])
+                    mx_pass(s1bank[(i, wo_units[k - 1][1])], "a", i, wo_units[k - 1])
         load_x(0)
         load_attn(2)
         load_x(1)
@@ -275,22 +289,21 @@ def tile_transformerblocktpu_pb_l_kernel(tc, attn, x, w_o, rms2_scale, w_gate, w
                 mean_square(i - 1)
             if i < LAGS[0]:
                 for rep in range(24 // LAGS[0]):
-                    bg_item(BG_RAMP)
+                    bg_item(BG_RAMP, True)
             else:
                 for rep in range(len(LAGS) + (1 if i < LAGS[0] + LEAD else 0)):
-                    bg_item(BG_WOVEN)
+                    bg_item(BG_WOVEN, True)
             if 2 <= i < NT:
                 stage1_mm(i)
             if 0 <= i - DN < NT:
                 norm(i - DN)
             if i < NT:
                 stage1_add(i, 0)
-            if 1 <= i and i + 1 < NT:
-                quant_attn(i + 1)
             if i < NT:
                 stage1_add(i, 1)
-            if 0 <= i - DN - 1 < NT:
-                quant_h(i - DN - 1)
+            if i >= 1 and i - 1 in runs:
+                quant_run(runs[i - 1])
+            flush()
             if i < NT:
                 stage1_add(i, 2)
                 nc.sync.dma_start(out=xmid_out[i * P:(i + 1) * P, :], in_=xmid[i][:])
@@ -306,12 +319,12 @@ def tile_transformerblocktpu_pb_l_kernel(tc, attn, x, w_o, rms2_scale, w_gate, w
             for job in held:
                 stage2_mul_store(*job)
             srcs = []
-            if i + 2 < NT:
-                srcs.append(("a", i + 2))
             if 0 <= i - DN < NT:
                 srcs.append(("h", i - DN))
+            if i + 2 < NT:
+                srcs.append(("a", i + 2))
             if srcs:
-                transposes(srcs)
+                runs[i] = transposes(srcs)
             if i == 0:
                 for n in range(NWO):
                     gb = bank()

from contextlib import ExitStack

import concourse.mybir as mybir
from concourse.masks import make_identity

F32 = mybir.dt.float32
BF16 = mybir.dt.bfloat16
U32 = mybir.dt.uint32
U8 = mybir.dt.uint8
FP8X4 = mybir.dt.float8_e4m3fn_x4
ALU = mybir.AluOpType
ACT = mybir.ActivationFunctionType

TOKENS, D, M = 3072, 1536, 6144
EPS = 1e-6
FLOPS = 2 * TOKENS * D * D + 2 * 2 * TOKENS * D * M

P = 128
PACK = 4
K_PASS = P * PACK
PASSES = D // K_PASS
NT = TOKENS // P
CH = 512
NCH = M // CH
NWO = D // CH

LAGS = (6,)
DN = 2
BG_RAMP = "s"
BG_WOVEN = "s"
BG_REST = "v"
LEAD = 6
ACOD_BUFS = {4: 1, 2: 3, 1: 2}
RAW_BUFS = 6
CODE_BUFS = 24
SG_BUFS = 6


def tile_transformerblocktpu_pb_l_kernel(tc, attn, x, w_o, rms2_scale, w_gate, w_up, out_0, out_1):
    nc = tc.nc
    attn2 = attn.flatten_outer_dims()
    x2 = x.flatten_outer_dims()
    xmid_out = out_0.flatten_outer_dims()
    g_out = out_1.flatten_outer_dims()

    with ExitStack() as ctx:
        const = ctx.enter_context(tc.tile_pool(name="const", bufs=1))
        hpool = ctx.enter_context(tc.tile_pool(name="hcodes", bufs=1))
        wpool = ctx.enter_context(tc.tile_pool(name="weights", bufs=1))
        apool = ctx.enter_context(tc.tile_pool(name="stage1", bufs=1))
        opool = ctx.enter_context(tc.tile_pool(name="outs", bufs=1))
        psum = ctx.enter_context(tc.psum_pool(name="psum", bufs=8))
        ctx.enter_context(tc.manual_schedule())

        def bank():
            return psum.tile([P, CH], F32, name="bank")

        ident = const.tile([P, P], F32, name="ident")
        make_identity(nc, ident[:])
        ones = const.tile([P, P], BF16, name="ones")
        nc.gpsimd.memset(ones[:], 1.0)
        neg_half = const.tile([P, 1], F32, name="neg_half")
        nc.gpsimd.memset(neg_half[:], -0.5)
        gain_row = apool.tile([P, D], BF16, name="hb", bufs=2)
        nc.gpsimd.memset(gain_row[:], 0.0)
        gain_bc = const.tile([P, D], BF16, name="gain_bc")
        junk = const.tile([P, D], BF16, name="junk")
        warm = const.tile([P, 1], F32, name="warm")
        nc.scalar.activation(out=warm[:], in_=neg_half[:], func=ACT.Silu)

        units = {}
        planes = {}

        def unit_src(key):
            mat, c, g = key
            w = {"o": w_o, "g": w_gate, "u": w_up}[mat]
            return w[g * K_PASS:(g + 1) * K_PASS, c * CH:(c + 1) * CH].rearrange("(p j) w -> p j w", j=PACK)

        def unit_load(key):
            raw = wpool.tile([P, PACK, CH], BF16, name="wraw", bufs=RAW_BUFS)
            nc.sync.dma_start(out=raw[:], in_=unit_src(key))
            units[key] = {"raw": raw}

        def unit_group(key, eng, lo, hi):
            u = units[key]
            if "grp" not in u:
                u["grp"] = wpool.tile([P, CH, PACK], BF16, name="wgrp", bufs=3, align_bytes=64)
            dst = u["grp"][:, lo:hi, :]
            src = u["raw"][:, :, lo:hi].rearrange("p j w -> p w j")
            if eng == "v":
                nc.vector.tensor_copy(out=dst, in_=src)
            elif eng == "s":
                nc.scalar.copy(out=dst, in_=src)
            else:
                nc.gpsimd.tensor_scalar(out=dst, in0=src, scalar1=1.0, scalar2=0.0, op0=ALU.mult, op1=ALU.add)

        def unit_quant(key):
            u = units[key]
            mat, c, g = key
            if (mat, c) not in planes:
                planes[(mat, c)] = wpool.tile([P, CH], U8, name="wscale", bufs=CODE_BUFS // PASSES, align_bytes=64)
            u["codes"] = wpool.tile([P, CH], U32, name="wcode", bufs=CODE_BUFS, align_bytes=64)
            u["scales"] = planes[(mat, c)][PACK * g:P, :]
            nc.vector.quantize_mx(out=u["codes"][:].bitcast(FP8X4), scales=u["scales"],
                                  in_=u["grp"][:].rearrange("p w j -> p (w j)"))

        araw, xraw, xmid, hb, tokcodes, runs, rstd = {}, {}, {}, {}, {}, {}, {}

        def load_attn(i):
            araw[i] = apool.tile([P, D], BF16, name="araw", bufs=3)
            nc.sync.dma_start(out=araw[i][:], in_=attn2[i * P:(i + 1) * P, :])

        def load_x(i):
            xraw[i] = apool.tile([P, D], BF16, name="xraw", bufs=3)
            nc.sync.dma_start(out=xraw[i][:], in_=x2[i * P:(i + 1) * P, :])

        def transposes(srcs):
            grp = apool.tile([P, 2 * PASSES, P, PACK], BF16, name="grp", bufs=2, align_bytes=64)
            gw = grp[:].bitcast(F32)
            items = [(kind, i, g) for kind, i in srcs for g in range(PASSES)]
            for b0 in range(0, len(items), 2):
                pair = items[b0:b0 + 2]
                bk = bank()
                bv = bk[:].rearrange("p (q r) -> p q r", r=P)
                for q, (kind, i, g) in enumerate(pair):
                    words = (araw[i] if kind == "a" else hb[i])[:].bitcast(F32)
                    for u in range(2):
                        nc.tensor.transpose(bv[:, 2 * q + u, :], words[:, 256 * g + u:256 * (g + 1):2], ident[:])
                n = len(pair)
                nc.scalar.copy(out=gw[:, b0:b0 + n, :, :], in_=bv[:, 0:2 * n, :].rearrange("p (g u) r -> p g r u", u=2))
            return (grp, items)

        def quant_run(run):
            grp, items = run
            n = len(items)
            first = 4 if n == 6 else 2
            keep = items[0][0] == "h"
            pool = hpool if keep else apool
            for lo, hi in ((0, first), (first, n)):
                w = hi - lo
                if keep and lo == 0:
                    cod = hpool.tile([P, w, P], U32, name="hcod%d" % items[0][1], align_bytes=64)
                    sca = hpool.tile([P, w * P], U8, name="hsca%d" % items[0][1], align_bytes=64)
                elif keep and n == 3:
                    cod = hpool.tile([P, w, P], U32, name="hcodb%d" % items[0][1], align_bytes=64)
                    sca = hpool.tile([P, w * P], U8, name="hscab%d" % items[0][1], align_bytes=64)
                else:
                    cod = apool.tile([P, w, P], U32, name="acod%d" % w, bufs=ACOD_BUFS[w], align_bytes=64)
                    sca = apool.tile([P, w * P], U8, name="asca%d" % w, bufs=ACOD_BUFS[w], align_bytes=64)
                nc.vector.quantize_mx(out=cod[:].rearrange("p g r -> p (g r)").bitcast(FP8X4), scales=sca[:],
                                      in_=grp[:, lo:hi, :, :].rearrange("p g r t -> p (g r t)"))
                for s in range(lo, hi):
                    kind, i, g = items[s]
                    tokcodes[(kind, i, g)] = (cod[:, s - lo, :], sca[:, (s - lo) * P:(s - lo + 1) * P])

        def mx_pass(out, kind, i, key):
            g = key[2]
            u = units[key]
            lcod, lsca = tokcodes[(kind, i, g)]
            nc.tensor.matmul_mx(out=out[:], lhsT=lcod.bitcast(FP8X4), lhsT_scale=lsca,
                                rhs=u["codes"][:].bitcast(FP8X4), rhs_scale=u["scales"],
                                start=(g == 0), stop=(g == PASSES - 1))

        def mx_group(out, kind, i, keys):
            for key in keys:
                mx_pass(out, kind, i, key)

        s1bank = {}

        def stage1_mm(i):
            for n in range(NWO):
                s1bank[(i, n)] = bank()
                mx_group(s1bank[(i, n)], "a", i, [("o", n, g) for g in range(PASSES)])

        def stage1_add(i, n):
            if n == 0:
                xmid[i] = apool.tile([P, D], F32, name="xmid", bufs=4)
            cols = slice(n * CH, (n + 1) * CH)
            nc.vector.tensor_tensor(out=xmid[i][:, cols], in0=s1bank[(i, n)][:], in1=xraw[i][:, cols], op=ALU.add)

        def mean_square(i):
            ssq = apool.tile([P, 1], F32, name="ssq", bufs=4)
            nc.scalar.activation(out=junk[:], in_=xmid[i][:], func=ACT.Square, accum_out=ssq[:])
            ms = apool.tile([P, 1], F32, name="ms", bufs=4)
            nc.gpsimd.tensor_scalar(out=ms[:], in0=ssq[:], scalar1=1.0 / D, scalar2=EPS, op0=ALU.mult, op1=ALU.add)
            rstd[i] = apool.tile([P, 1], F32, name="rstd", bufs=4)
            nc.gpsimd.tensor_tensor(out=rstd[i][:], in0=ms[:], in1=neg_half[:], op=ALU.pow)

        def norm(i):
            hb[i] = apool.tile([P, D], BF16, name="hb", bufs=2)
            nc.vector.scalar_tensor_tensor(out=hb[i][:], in0=xmid[i][:], scalar=rstd[i][:, 0:1],
                                           in1=gain_bc[:], op0=ALU.mult, op1=ALU.mult)

        def stage2_mm(c, i):
            bg, bu = bank(), bank()
            mx_group(bg, "h", i, [("g", c, g) for g in range(PASSES)])
            mx_group(bu, "h", i, [("u", c, g) for g in range(PASSES)])
            return bg, bu

        def stage2_silu(bg):
            sg = opool.tile([P, CH], F32, name="sg", bufs=SG_BUFS)
            nc.scalar.activation(out=sg[:], in_=bg[:], func=ACT.Silu)
            return sg

        def stage2_mul_store(c, i, bu, sg):
            nc.vector.tensor_tensor(out=sg[:], in0=bu[:], in1=sg[:], op=ALU.mult)
            nc.sync.dma_start(out=g_out[i * P:(i + 1) * P, c * CH:(c + 1) * CH], in_=sg[:])

        stream = [(m, c, g) for c in range(NCH) for m in ("g", "u") for g in range(PASSES)]
        pos = {"load": 0, "item": 0, "live": NWO * PASSES, "turn": 0}

        def bg_load():
            if pos["load"] < len(stream):
                unit_load(stream[pos["load"]])
                pos["load"] += 1

        pending = {"keys": []}

        def flush():
            for key in pending["keys"]:
                unit_quant(key)
            pending["keys"] = []

        def bg_item(engines, defer=False):
            k = pos["item"]
            if k > 4 * len(stream):
                return
            u, part = k // 4, k % 4
            if part == 0 and pos["live"] >= CODE_BUFS:
                return
            if part == 0 and u >= 1:
                if defer:
                    pending["keys"] = pending["keys"] + [stream[u - 1]]
                else:
                    unit_quant(stream[u - 1])
                pos["live"] += 1
            elif part in (1, 2) and u < len(stream):
                eng = engines[pos["turn"] % len(engines)]
                pos["turn"] += 1
                unit_group(stream[u], eng, (part - 1) * CH // 2, part * CH // 2)
            elif part == 3:
                bg_load()
            pos["item"] += 1

        def need_chunk(c, engines):
            while pos["item"] < 24 * (c + 1) + 1:
                bg_item(engines)

        wo_units = [("o", n, g) for g in range(PASSES) for n in range(NWO)]
        load_attn(0)
        load_attn(1)
        for key in wo_units[0:RAW_BUFS]:
            unit_load(key)
        runs[-1] = transposes([("a", 0), ("a", 1)])
        for i in range(2):
            for n in range(NWO):
                s1bank[(i, n)] = bank()
        for k in range(len(wo_units) + 1):
            if k < len(wo_units):
                unit_group(wo_units[k], "v", 0, CH // 2)
                unit_group(wo_units[k], "s", CH // 2, CH)
            if k + RAW_BUFS < len(wo_units):
                unit_load(wo_units[k + RAW_BUFS])
            if k == 1:
                quant_run(runs[-1])
            if k >= 1:
                unit_quant(wo_units[k - 1])
                for i in range(2):
                    mx_pass(s1bank[(i, wo_units[k - 1][1])], "a", i, wo_units[k - 1])
        load_x(0)
        load_attn(2)
        load_x(1)
        nc.sync.dma_start(out=gain_row[0:1, :], in_=rms2_scale.rearrange("(o d) -> o d", o=1))
        bg_load()
        bg_load()

        done = {}
        for i in range(NT + DN + 1):
            if i + 3 < NT:
                load_attn(i + 3)
            if i + 2 < NT:
                load_x(i + 2)
            if i < RAW_BUFS - 2:
                bg_load()
            now = [(c, i - lag) for c, lag in enumerate(LAGS) if 0 <= i - lag < NT and i - lag <= i - DN - 2]
            for c, t in now:
                need_chunk(c, BG_RAMP)
            if 0 <= i - 1 < NT:
                mean_square(i - 1)
            if i < LAGS[0]:
                for rep in range(24 // LAGS[0]):
                    bg_item(BG_RAMP, True)
            else:
                for rep in range(len(LAGS) + (1 if i < LAGS[0] + LEAD else 0)):
                    bg_item(BG_WOVEN, True)
            if 2 <= i < NT:
                stage1_mm(i)
            if 0 <= i - DN < NT:
                norm(i - DN)
            if i < NT:
                stage1_add(i, 0)
            if i < NT:
                stage1_add(i, 1)
            if i >= 1 and i - 1 in runs:
                quant_run(runs[i - 1])
            flush()
            if i < NT:
                stage1_add(i, 2)
                nc.sync.dma_start(out=xmid_out[i * P:(i + 1) * P, :], in_=xmid[i][:])
            if i == NT - 1:
                pos["live"] -= NWO * PASSES
            held = []
            for c, t in now:
                bg, bu = stage2_mm(c, t)
                held.append((c, t, bu, stage2_silu(bg)))
                done[(c, t)] = True
                if t == NT - 1:
                    pos["live"] -= 2 * PASSES
            for job in held:
                stage2_mul_store(*job)
            srcs = []
            if 0 <= i - DN < NT:
                srcs.append(("h", i - DN))
            if i + 2 < NT:
                srcs.append(("a", i + 2))
            if srcs:
                runs[i] = transposes(srcs)
            if i == 0:
                for n in range(NWO):
                    gb = bank()
                    nc.tensor.matmul(out=gb[:], lhsT=ones[:], rhs=gain_row[:, n * CH:(n + 1) * CH], start=True, stop=True)
                    nc.scalar.copy(out=gain_bc[:, n * CH:(n + 1) * CH], in_=gb[:])

        for c in range(NCH):
            for t in range(NT):
                if (c, t) in done:
                    continue
                need_chunk(c, BG_REST)
                bg, bu = stage2_mm(c, t)
                sg = stage2_silu(bg)
                stage2_mul_store(c, t, bu, sg)
                if t == NT - 1:
                    pos["live"] -= 2 * PASSES
                bg_item(BG_REST)
